import numpy as np
import ml_dtypes


def mxq(x, axis, fmt="e4m3"):
    dtype, down = {"e4m3": (ml_dtypes.float8_e4m3fn, 7), "e5m2": (ml_dtypes.float8_e5m2, 14)}[fmt]
    v = np.moveaxis(np.asarray(x, np.float32).astype(ml_dtypes.bfloat16).astype(np.float64), axis, -1)
    blocks = v.reshape(v.shape[:-1] + (-1, 32))
    amax = np.abs(blocks).max(-1, keepdims=True)
    byte = np.maximum(np.where(amax > 0, np.frexp(amax)[1] - 1 + 127, 0) - down, 1)
    scale = np.exp2(byte - 127.0)
    codes = (blocks / scale).astype(np.float32).astype(dtype).astype(np.float64)
    return np.moveaxis((codes * scale).reshape(v.shape), -1, axis)


WIDE = False


def mx_kscale(k):
    if not WIDE:
        return np.ones(k)
    levels = np.array([10, -10, 5, -5, 0])
    a = np.random.permutation(np.resize(levels, k // 512 * 4)).reshape(k // 512, 4)
    idx = np.arange(k)
    return np.exp2(a[idx // 512, idx % 128 // 32])


BF16 = ml_dtypes.bfloat16


def bf(x):
    return np.asarray(x, np.float32).astype(BF16)


def f64(x):
    return np.asarray(x).astype(np.float64)


B, T, H, HD, W, G = 1, 4096, 4, 128, 512, 512
D = H * HD
NW = T // W


def setup_inputs():
    s = mx_kscale(D)
    return {"x": bf(np.random.standard_normal((B, T, D)) * s),
            "Wv": bf(np.random.standard_normal((D, D)) * 2.0 / np.sqrt(D) / s[None, :]),
            "q": bf(np.random.standard_normal((B, H, T, HD)) * 1.4),
            "k": bf(np.random.standard_normal((B, H, T, HD)) * 1.4)}


def reference(x, Wv, q, k):
    scale = HD ** -0.5
    v = (mxq(f64(x), 2, "e4m3") @ mxq(f64(Wv), 1, "e4m3").T).reshape(B, T, H, HD).transpose(0, 2, 1, 3)
    qw = f64(q).reshape(B, H, NW, W, HD)
    kk = f64(k)
    kw = kk.reshape(B, H, NW, W, HD)
    kg = kk[:, :, :G, :]
    s_g = (qw @ kg[:, :, None].transpose(0, 1, 2, 4, 3)) * scale
    s_l = (qw @ kw.transpose(0, 1, 2, 4, 3)) * scale
    s = np.concatenate([s_g, s_l], axis=-1)
    e = np.exp(s - s.max(-1, keepdims=True))
    vq = mxq(v, 2, "e4m3")
    o = (mxq(e[..., :G], 4, "e4m3") @ vq[:, :, None, :G, :]) + (mxq(e[..., G:], 4, "e4m3") @ vq.reshape(B, H, NW, W, HD))
    o = o / e.sum(-1, keepdims=True)
    return o.reshape(B, H, T, HD).transpose(0, 2, 1, 3).reshape(B, T, D)

@@ -1,0 +1,318 @@
+from contextlib import ExitStack
+
+import concourse.mybir as mybir
+from concourse.masks import make_identity
+
+BF16 = mybir.dt.bfloat16
+F32 = mybir.dt.float32
+U32 = mybir.dt.uint32
+U8 = mybir.dt.uint8
+FP8X4 = mybir.dt.float8_e4m3fn_x4
+EXP = mybir.ActivationFunctionType.Exp
+MAX = mybir.AluOpType.max
+MULT = mybir.AluOpType.mult
+ADD = mybir.AluOpType.add
+AXIS_X = mybir.AxisListType.X
+
+P = 128
+PACK = 4
+T = 4096
+H = 4
+HD = 128
+D = H * HD
+W = 512
+NW = T // W
+TILES = W // P
+SCALE = HD**-0.5
+
+N_TILES = NW * TILES * H
+
+FLOPS = 2 * T * D * D + 2 * (2 * H * T * (2 * W) * HD)
+
+
+def tile_hybridattention_pa_t_kernel(tc, x, Wv, q, k, out):
+    nc = tc.nc
+    with ExitStack() as ctx:
+        const = ctx.enter_context(tc.tile_pool(name="const", bufs=1))
+        keep = ctx.enter_context(tc.tile_pool(name="keep", bufs=1))
+        raw = ctx.enter_context(tc.tile_pool(name="raw", bufs=2))
+        work = ctx.enter_context(tc.tile_pool(name="work", bufs=6))
+        small = ctx.enter_context(tc.tile_pool(name="small", bufs=6))
+        psum_s = ctx.enter_context(tc.psum_pool(name="psum_s", bufs=4))
+        psum_t = ctx.enter_context(tc.psum_pool(name="psum_t", bufs=3))
+        psum_o = ctx.enter_context(tc.psum_pool(name="psum_o", bufs=1))
+        ctx.enter_context(tc.manual_schedule())
+
+        ident_bf16 = const.tile([P, P], BF16)
+        make_identity(nc, ident_bf16[:])
+        ident_f32 = const.tile([P, P], F32)
+        make_identity(nc, ident_f32[:])
+
+
+        def flip_words(rows, n):
+            words = rows.bitcast(F32)
+            flipped = psum_t.tile([P, 2, 2, P], F32, tag="bank")
+            for g in range(n):
+                for u in range(2):
+                    nc.tensor.transpose(
+                        out=flipped[:, g, u, :], in_=words[:, g, u * P : (u + 1) * P], identity=ident_f32[:]
+                    )
+            return flipped
+
+        def regroup_words(copy, flipped, n):
+            grouped = work.tile([P, 2, P, PACK], BF16, align_bytes=64)
+            copy(out=grouped[:, 0:n].bitcast(F32), in_=flipped[:, 0:n].rearrange("p g u c -> p g c u"))
+            return grouped
+
+        def quantise_words(grouped, n, codes, scales):
+            nc.vector.quantize_mx(
+                out=codes.rearrange("p g c -> p (g c)").bitcast(FP8X4),
+                scales=scales.rearrange("p g c -> p (g c)"),
+                in_=grouped[:, 0:n].rearrange("p g c t -> p (g c t)"),
+            )
+
+        qT = [keep.tile([P, H, W], BF16, name="qT%d" % w) for w in range(NW)]
+        kT = [keep.tile([P, H, W], BF16, name="kT%d" % w) for w in range(NW)]
+        x_codes = [keep.tile([P, TILES, P], U32, name="x_codes%d" % w, align_bytes=64) for w in range(NW)]
+        x_scales = [keep.tile([P, TILES, P], U8, name="x_scales%d" % w, align_bytes=64) for w in range(NW)]
+        v_codes = [keep.tile([P, H, HD], U32, name="v_codes%d" % w, align_bytes=64) for w in range(NW)]
+        v_scales = [keep.tile([P, H, HD], U8, name="v_scales%d" % w, align_bytes=64) for w in range(NW)]
+        q_raw = {}
+        k_raw = {}
+        x_raw = {}
+        in_psum = {}
+        in_sbuf = {}
+
+        def load_qk(w):
+            rows = slice(w * W, (w + 1) * W)
+            q_raw[w] = raw.tile([P, H, TILES * HD], BF16, name="q_raw")
+            nc.sync.dma_start(
+                out=q_raw[w][:], in_=q[0, :, rows, :].rearrange("h (p j) d -> p h (j d)", j=TILES)
+            )
+            k_raw[w] = raw.tile([P, H, TILES * HD], BF16, name="k_raw")
+            for h in range(H):
+                nc.sync.dma_start(
+                    out=k_raw[w][:, h, :].rearrange("p (j d) -> p j d", d=HD),
+                    in_=k[0, h, rows, :].rearrange("(j p) d -> p j d", p=P),
+                )
+
+        def load_x(w):
+            x_raw[w] = raw.tile([P, TILES, D], BF16, name="x_raw")
+            nc.sync.dma_start(
+                out=x_raw[w][:].rearrange("p (u e) f -> p u (e f)", e=2),
+                in_=x[0, w * W : (w + 1) * W, :].rearrange("(u p e) f -> p u (e f)", u=2, e=2),
+            )
+
+        def turn_qk(w, h):
+            turned = psum_t.tile([P, 2, W], BF16, tag="bank")
+            for i, src in enumerate((q_raw[w], k_raw[w])):
+                for j in range(TILES):
+                    cols = slice(j * P, (j + 1) * P)
+                    nc.tensor.transpose(out=turned[:, i, cols], in_=src[:, h, cols], identity=ident_bf16[:])
+            in_psum["qk"] = turned
+
+        def keep_qk(w, h):
+            nc.vector.tensor_copy(out=qT[w][:, h, :], in_=in_psum["qk"][:, 0, :])
+            nc.vector.tensor_copy(out=kT[w][:, h, :], in_=in_psum["qk"][:, 1, :])
+
+        def flip_x(w, t):
+            in_psum["x"] = flip_words(x_raw[w][:, t : t + 1, :], 1)
+
+        def regroup_x():
+            in_sbuf["x"] = regroup_words(nc.vector.tensor_copy, in_psum["x"], 1)
+
+        def quantise_x(w, t):
+            quantise_words(in_sbuf["x"], 1, x_codes[w][:, t : t + 1, :], x_scales[w][:, t : t + 1, :])
+
+        def project_v(w, h):
+            v_ps = psum_t.tile([P, PACK, HD], F32, tag="bank")
+            for t in range(PACK):
+                nc.tensor.matmul_mx(
+                    out=v_ps[:, t, :],
+                    lhsT=x_codes[w][:, t, :].bitcast(FP8X4),
+                    lhsT_scale=x_scales[w][:, t, :],
+                    rhs=wv_codes[:, h, :].bitcast(FP8X4),
+                    rhs_scale=wv_scales[:, h, :],
+                    start=True,
+                    stop=True,
+                )
+            in_psum["v"] = v_ps
+
+        def round_v():
+            v_grouped = work.tile([P, HD, PACK], BF16, align_bytes=64)
+            nc.scalar.copy(out=v_grouped[:], in_=in_psum["v"][:].rearrange("p t d -> p d t"))
+            in_sbuf["v"] = v_grouped
+
+        def quantise_v(w, h):
+            nc.vector.quantize_mx(
+                out=v_codes[w][:, h, :].bitcast(FP8X4),
+                scales=v_scales[w][:, h, :],
+                in_=in_sbuf["v"][:].rearrange("p d t -> p (d t)"),
+            )
+
+        def where(n):
+            return n // (TILES * H), (n // H) % TILES, n % H
+
+        def key_windows(w):
+            return (0,) if w == 0 else (0, w)
+
+        s_ps = {}
+        row_max = {}
+        bias = {}
+        sums = {}
+        e = {}
+        e_flipped = {}
+        e_grouped = {}
+        e_codes = {}
+        e_scales = {}
+        o_ps = {}
+
+        def scores(n):
+            w, j, h = where(n)
+            s_ps[n] = []
+            for kw in key_windows(w):
+                bank = psum_s.tile([P, W], F32)
+                nc.tensor.matmul(
+                    out=bank[:], lhsT=qT[w][:, h, j * P : (j + 1) * P], rhs=kT[kw][:, h, :], start=True, stop=True
+                )
+                s_ps[n].append(bank)
+
+        def row_maxima(n):
+            row_max[n] = small.tile([P, 2], F32, name="row_max")
+            for i, bank in enumerate(s_ps[n]):
+                nc.vector.tensor_reduce(out=row_max[n][:, i : i + 1], in_=bank[:], axis=AXIS_X, op=MAX)
+
+        def exp_bias(n):
+            last = len(s_ps[n]) - 1
+            bias[n] = small.tile([P, 1], F32, name="bias")
+            nc.vector.tensor_scalar(
+                out=bias[n][:],
+                in0=row_max[n][:, 0:1],
+                scalar1=row_max[n][:, last : last + 1],
+                scalar2=-SCALE,
+                op0=MAX,
+                op1=MULT,
+            )
+
+        def exponentials(n):
+            w, j, h = where(n)
+            if h == 0:
+                sums[w, j] = small.tile([P, H, 2], F32, name="sums")
+            e[n] = work.tile([P, 2, W], BF16, name="e")
+            for i, bank in enumerate(s_ps[n]):
+                nc.scalar.activation(
+                    out=e[n][:, i, :],
+                    in_=bank[:],
+                    func=EXP,
+                    bias=bias[n][:],
+                    scale=SCALE,
+                    accum_out=sums[w, j][:, h, i : i + 1],
+                )
+
+        def flip_e(n):
+            n_kw = len(s_ps[n])
+            e_flipped[n] = flip_words(e[n][:, 0:n_kw, :], n_kw)
+
+        def regroup_e(n):
+            e_grouped[n] = regroup_words(nc.scalar.copy, e_flipped[n], len(s_ps[n]))
+
+        def quantise_e(n):
+            n_kw = len(s_ps[n])
+            e_codes[n] = work.tile([P, 2, P], U32, name="e_codes", align_bytes=64)
+            e_scales[n] = work.tile([P, 2, P], U8, name="e_scales", align_bytes=64)
+            quantise_words(e_grouped[n], n_kw, e_codes[n][:, 0:n_kw, :], e_scales[n][:, 0:n_kw, :])
+
+        def weigh_values(n):
+            w, j, h = where(n)
+            if h == 0:
+                o_ps[w, j] = psum_o.tile([P, H, HD], F32, name="o_ps")
+            windows = key_windows(w)
+            for i, kw in enumerate(windows):
+                nc.tensor.matmul_mx(
+                    out=o_ps[w, j][:, h, :],
+                    lhsT=e_codes[n][:, i, :].bitcast(FP8X4),
+                    lhsT_scale=e_scales[n][:, i, :],
+                    rhs=v_codes[kw][:, h, :].bitcast(FP8X4),
+                    rhs_scale=v_scales[kw][:, h, :],
+                    start=(i == 0),
+                    stop=(i == len(windows) - 1),
+                )
+
+        def divide_and_store(w, j):
+            n_kw = len(key_windows(w))
+            total = small.tile([P, H], F32)
+            nc.vector.tensor_reduce(out=total[:], in_=sums[w, j][:, :, 0:n_kw], axis=AXIS_X, op=ADD)
+            inverse = small.tile([P, H], F32)
+            nc.vector.reciprocal(out=inverse[:], in_=total[:])
+            o_sb = work.tile([P, H, HD], F32)
+            nc.vector.tensor_tensor(
+                out=o_sb[:], in0=o_ps[w, j][:], in1=inverse[:].unsqueeze(2).to_broadcast([P, H, HD]), op=MULT
+            )
+            nc.sync.dma_start(
+                out=out[0, w * W : (w + 1) * W, :].rearrange("(p j) f -> j p f", j=TILES)[j],
+                in_=o_sb[:].rearrange("p h d -> p (h d)"),
+            )
+
+        wv_raw = const.tile([P, TILES, D], BF16)
+        load_x(0)
+        nc.sync.dma_start(out=wv_raw[:], in_=Wv.rearrange("(o p) f -> p o f", p=P))
+        wv_codes = const.tile([P, TILES, P], U32, align_bytes=64)
+        wv_scales = const.tile([P, TILES, P], U8, align_bytes=64)
+        for o in range(0, TILES, 2):
+            wv_grouped = regroup_words(nc.scalar.copy, flip_words(wv_raw[:, o : o + 2, :], 2), 2)
+            quantise_words(wv_grouped, 2, wv_codes[:, o : o + 2, :], wv_scales[:, o : o + 2, :])
+
+        def if_tile(stage, n):
+            if 0 <= n < N_TILES:
+                stage(n)
+
+        def chain_started(n, first_round, ahead):
+            w, j, h = where(n)
+            return (w + ahead, j) if h == first_round and 0 <= w + ahead < NW else None
+
+        def x_tile(n):
+            return chain_started(n, 0, 2)
+
+        def v_head(n):
+            return chain_started(n, 1, 1)
+
+        def qk_head(n):
+            return chain_started(n, 2, 1)
+
+        for n in range(-2 * TILES * H, N_TILES + 4):
+            w, j, h = where(n)
+            if h == 0 and j == 0:
+                if w + 2 < NW:
+                    load_qk(w + 2)
+                if w + 3 < NW:
+                    load_x(w + 3)
+
+            if_tile(scores, n + 1)
+            if_tile(flip_e, n - 1)
+
+            if_tile(row_maxima, n)
+            if_tile(exp_bias, n)
+            if_tile(quantise_e, n - 3)
+            if h == H - 1 and n - H >= 0:
+                divide_and_store(*where(n - H)[0:2])
+            if qk_head(n - 1):
+                keep_qk(*qk_head(n - 1))
+            if x_tile(n - 1):
+                regroup_x()
+            if x_tile(n - 3):
+                quantise_x(*x_tile(n - 3))
+            if v_head(n - 3):
+                quantise_v(*v_head(n - 3))
+
+            if_tile(exponentials, n)
+            if_tile(regroup_e, n - 1)
+            if v_head(n - 1):
+                round_v()
+
+            if_tile(weigh_values, n - 3)
+            if v_head(n):
+                project_v(*v_head(n))
+            if x_tile(n):
+                flip_x(*x_tile(n))
+            if qk_head(n):
+                turn_qk(*qk_head(n))

@@ -166,6 +166,8 @@ def tile_hybridattention_pa_t_kernel(tc, x, Wv, q, k, out):
         e_codes = {}
         e_scales = {}
         o_ps = {}
+        total = {}
+        inverse = {}
 
         def scores(n):
             w, j, h = where(n)
@@ -238,15 +240,22 @@ def tile_hybridattention_pa_t_kernel(tc, x, Wv, q, k, out):
                     stop=(i == len(windows) - 1),
                 )
 
-        def divide_and_store(w, j):
+        def add_sums(w, j):
             n_kw = len(key_windows(w))
-            total = small.tile([P, H], F32)
-            nc.vector.tensor_reduce(out=total[:], in_=sums[w, j][:, :, 0:n_kw], axis=AXIS_X, op=ADD)
-            inverse = small.tile([P, H], F32)
-            nc.vector.reciprocal(out=inverse[:], in_=total[:])
+            total[w, j] = small.tile([P, H], F32, name="total")
+            nc.vector.tensor_reduce(out=total[w, j][:], in_=sums[w, j][:, :, 0:n_kw], axis=AXIS_X, op=ADD)
+
+        def invert_sums(w, j):
+            inverse[w, j] = small.tile([P, H], F32, name="inverse")
+            nc.vector.reciprocal(out=inverse[w, j][:], in_=total[w, j][:])
+
+        def divide_and_store(w, j):
             o_sb = work.tile([P, H, HD], F32)
             nc.vector.tensor_tensor(
-                out=o_sb[:], in0=o_ps[w, j][:], in1=inverse[:].unsqueeze(2).to_broadcast([P, H, HD]), op=MULT
+                out=o_sb[:],
+                in0=o_ps[w, j][:],
+                in1=inverse[w, j][:].unsqueeze(2).to_broadcast([P, H, HD]),
+                op=MULT,
             )
             nc.sync.dma_start(
                 out=out[0, w * W : (w + 1) * W, :].rearrange("(p j) f -> j p f", j=TILES)[j],
@@ -290,15 +299,20 @@ def tile_hybridattention_pa_t_kernel(tc, x, Wv, q, k, out):
             if_tile(scores, n + 1)
             if_tile(flip_e, n - 1)
 
+            finished = where(n - H)[0:2] if h == H - 1 and n - H >= 0 else None
             if_tile(row_maxima, n)
-            if_tile(exp_bias, n)
+            if finished:
+                add_sums(*finished)
             if_tile(quantise_e, n - 3)
-            if h == H - 1 and n - H >= 0:
-                divide_and_store(*where(n - H)[0:2])
+            if finished:
+                invert_sums(*finished)
+            if_tile(exp_bias, n)
             if qk_head(n - 1):
                 keep_qk(*qk_head(n - 1))
             if x_tile(n - 1):
                 regroup_x()
+            if finished:
+                divide_and_store(*finished)
             if x_tile(n - 3):
                 quantise_x(*x_tile(n - 3))
             if v_head(n - 3):

@@ -59,9 +59,11 @@ def tile_hybridattention_pa_t_kernel(tc, x, Wv, q, k, out):
                     )
             return flipped
 
-        def regroup_words(copy, flipped, n):
+        def regroup_words(flipped, n):
             grouped = work.tile([P, 2, P, PACK], BF16, align_bytes=64)
-            copy(out=grouped[:, 0:n].bitcast(F32), in_=flipped[:, 0:n].rearrange("p g u c -> p g c u"))
+            nc.scalar.copy(
+                out=grouped[:, 0:n].bitcast(F32), in_=flipped[:, 0:n].rearrange("p g u c -> p g c u")
+            )
             return grouped
 
         def quantise_words(grouped, n, codes, scales):
@@ -71,8 +73,7 @@ def tile_hybridattention_pa_t_kernel(tc, x, Wv, q, k, out):
                 in_=grouped[:, 0:n].rearrange("p g c t -> p (g c t)"),
             )
 
-        qT = [keep.tile([P, H, W], BF16, name="qT%d" % w) for w in range(NW)]
-        kT = [keep.tile([P, H, W], BF16, name="kT%d" % w) for w in range(NW)]
+        qkT = [keep.tile([P, H, 2, W], BF16, name="qkT%d" % w) for w in range(NW)]
         x_codes = [keep.tile([P, TILES, P], U32, name="x_codes%d" % w, align_bytes=64) for w in range(NW)]
         x_scales = [keep.tile([P, TILES, P], U8, name="x_scales%d" % w, align_bytes=64) for w in range(NW)]
         v_codes = [keep.tile([P, H, HD], U32, name="v_codes%d" % w, align_bytes=64) for w in range(NW)]
@@ -112,14 +113,13 @@ def tile_hybridattention_pa_t_kernel(tc, x, Wv, q, k, out):
             in_psum["qk"] = turned
 
         def keep_qk(w, h):
-            nc.vector.tensor_copy(out=qT[w][:, h, :], in_=in_psum["qk"][:, 0, :])
-            nc.vector.tensor_copy(out=kT[w][:, h, :], in_=in_psum["qk"][:, 1, :])
+            nc.vector.tensor_copy(out=qkT[w][:, h], in_=in_psum["qk"][:])
 
         def flip_x(w, t):
             in_psum["x"] = flip_words(x_raw[w][:, t : t + 1, :], 1)
 
         def regroup_x():
-            in_sbuf["x"] = regroup_words(nc.vector.tensor_copy, in_psum["x"], 1)
+            in_sbuf["x"] = regroup_words(in_psum["x"], 1)
 
         def quantise_x(w, t):
             quantise_words(in_sbuf["x"], 1, x_codes[w][:, t : t + 1, :], x_scales[w][:, t : t + 1, :])
@@ -175,7 +175,11 @@ def tile_hybridattention_pa_t_kernel(tc, x, Wv, q, k, out):
             for kw in key_windows(w):
                 bank = psum_s.tile([P, W], F32)
                 nc.tensor.matmul(
-                    out=bank[:], lhsT=qT[w][:, h, j * P : (j + 1) * P], rhs=kT[kw][:, h, :], start=True, stop=True
+                    out=bank[:],
+                    lhsT=qkT[w][:, h, 0, j * P : (j + 1) * P],
+                    rhs=qkT[kw][:, h, 1, :],
+                    start=True,
+                    stop=True,
                 )
                 s_ps[n].append(bank)
 
@@ -216,7 +220,7 @@ def tile_hybridattention_pa_t_kernel(tc, x, Wv, q, k, out):
             e_flipped[n] = flip_words(e[n][:, 0:n_kw, :], n_kw)
 
         def regroup_e(n):
-            e_grouped[n] = regroup_words(nc.scalar.copy, e_flipped[n], len(s_ps[n]))
+            e_grouped[n] = regroup_words(e_flipped[n], len(s_ps[n]))
 
         def quantise_e(n):
             n_kw = len(s_ps[n])
@@ -241,13 +245,14 @@ def tile_hybridattention_pa_t_kernel(tc, x, Wv, q, k, out):
                 )
 
         def add_sums(w, j):
-            n_kw = len(key_windows(w))
             total[w, j] = small.tile([P, H], F32, name="total")
-            nc.vector.tensor_reduce(out=total[w, j][:], in_=sums[w, j][:, :, 0:n_kw], axis=AXIS_X, op=ADD)
+            nc.gpsimd.tensor_tensor(
+                out=total[w, j][:], in0=sums[w, j][:, :, 0], in1=sums[w, j][:, :, 1], op=ADD
+            )
 
         def invert_sums(w, j):
             inverse[w, j] = small.tile([P, H], F32, name="inverse")
-            nc.vector.reciprocal(out=inverse[w, j][:], in_=total[w, j][:])
+            nc.vector.reciprocal(out=inverse[w, j][:], in_=sums[w, j][:, :, 0] if w == 0 else total[w, j][:])
 
         def divide_and_store(w, j):
             o_sb = work.tile([P, H, HD], F32)
@@ -268,7 +273,7 @@ def tile_hybridattention_pa_t_kernel(tc, x, Wv, q, k, out):
         wv_codes = const.tile([P, TILES, P], U32, align_bytes=64)
         wv_scales = const.tile([P, TILES, P], U8, align_bytes=64)
         for o in range(0, TILES, 2):
-            wv_grouped = regroup_words(nc.scalar.copy, flip_words(wv_raw[:, o : o + 2, :], 2), 2)
+            wv_grouped = regroup_words(flip_words(wv_raw[:, o : o + 2, :], 2), 2)
             quantise_words(wv_grouped, 2, wv_codes[:, o : o + 2, :], wv_scales[:, o : o + 2, :])
 
         def if_tile(stage, n):
@@ -283,10 +288,10 @@ def tile_hybridattention_pa_t_kernel(tc, x, Wv, q, k, out):
             return chain_started(n, 0, 2)
 
         def v_head(n):
-            return chain_started(n, 1, 1)
+            return chain_started(n, 2, 1)
 
         def qk_head(n):
-            return chain_started(n, 2, 1)
+            return chain_started(n, 3, 1)
 
         for n in range(-2 * TILES * H, N_TILES + 4):
             w, j, h = where(n)
@@ -302,15 +307,11 @@ def tile_hybridattention_pa_t_kernel(tc, x, Wv, q, k, out):
             finished = where(n - H)[0:2] if h == H - 1 and n - H >= 0 else None
             if_tile(row_maxima, n)
             if finished:
-                add_sums(*finished)
-            if_tile(quantise_e, n - 3)
-            if finished:
                 invert_sums(*finished)
+            if_tile(quantise_e, n - 3)
             if_tile(exp_bias, n)
             if qk_head(n - 1):
                 keep_qk(*qk_head(n - 1))
-            if x_tile(n - 1):
-                regroup_x()
             if finished:
                 divide_and_store(*finished)
             if x_tile(n - 3):
@@ -320,8 +321,12 @@ def tile_hybridattention_pa_t_kernel(tc, x, Wv, q, k, out):
 
             if_tile(exponentials, n)
             if_tile(regroup_e, n - 1)
+            if x_tile(n - 1):
+                regroup_x()
             if v_head(n - 1):
                 round_v()
+            if h == H - 1 and 0 < w < NW:
+                add_sums(w, j)
 
             if_tile(weigh_values, n - 3)
             if v_head(n):

@@ -191,7 +191,7 @@ def tile_hybridattention_pa_t_kernel(tc, x, Wv, q, k, out):
         def exp_bias(n):
             last = len(s_ps[n]) - 1
             bias[n] = small.tile([P, 1], F32, name="bias")
-            nc.vector.tensor_scalar(
+            nc.gpsimd.tensor_scalar(
                 out=bias[n][:],
                 in0=row_max[n][:, 0:1],
                 scalar1=row_max[n][:, last : last + 1],

@@ -12,6 +12,7 @@ EXP = mybir.ActivationFunctionType.Exp
 MAX = mybir.AluOpType.max
 MULT = mybir.AluOpType.mult
 ADD = mybir.AluOpType.add
+POW = mybir.AluOpType.pow
 AXIS_X = mybir.AxisListType.X
 
 P = 128
@@ -25,9 +26,16 @@ NW = T // W
 TILES = W // P
 SCALE = HD**-0.5
 
-N_TILES = NW * TILES * H
+BANKS = 2
+ROUNDS = TILES * H
+ROUNDS_0 = ROUNDS // BANKS
+N_ROUNDS = ROUNDS_0 + (NW - 1) * ROUNDS
 
 FLOPS = 2 * T * D * D + 2 * (2 * H * T * (2 * W) * HD)
+
+
+def first_round(w):
+    return 0 if w == 0 else ROUNDS_0 + (w - 1) * ROUNDS
 
 
 def tile_hybridattention_pa_t_kernel(tc, x, Wv, q, k, out):
@@ -36,10 +44,13 @@ def tile_hybridattention_pa_t_kernel(tc, x, Wv, q, k, out):
         const = ctx.enter_context(tc.tile_pool(name="const", bufs=1))
         keep = ctx.enter_context(tc.tile_pool(name="keep", bufs=1))
         raw = ctx.enter_context(tc.tile_pool(name="raw", bufs=2))
-        work = ctx.enter_context(tc.tile_pool(name="work", bufs=6))
+        raw_x = ctx.enter_context(tc.tile_pool(name="raw_x", bufs=3))
+        prep = ctx.enter_context(tc.tile_pool(name="prep", bufs=2))
+        work = ctx.enter_context(tc.tile_pool(name="work", bufs=4))
         small = ctx.enter_context(tc.tile_pool(name="small", bufs=6))
-        psum_s = ctx.enter_context(tc.psum_pool(name="psum_s", bufs=4))
-        psum_t = ctx.enter_context(tc.psum_pool(name="psum_t", bufs=3))
+        psum_s = ctx.enter_context(tc.psum_pool(name="psum_s", bufs=5))
+        psum_e = ctx.enter_context(tc.psum_pool(name="psum_e", bufs=1))
+        psum_t = ctx.enter_context(tc.psum_pool(name="psum_t", bufs=1))
         psum_o = ctx.enter_context(tc.psum_pool(name="psum_o", bufs=1))
         ctx.enter_context(tc.manual_schedule())
 
@@ -47,30 +58,27 @@ def tile_hybridattention_pa_t_kernel(tc, x, Wv, q, k, out):
         make_identity(nc, ident_bf16[:])
         ident_f32 = const.tile([P, P], F32)
         make_identity(nc, ident_f32[:])
+        minus_one = const.tile([P, H], F32)
+        nc.gpsimd.memset(minus_one[:], -1.0)
 
-
-        def flip_words(rows, n):
+        def flip_words(pool, rows):
             words = rows.bitcast(F32)
-            flipped = psum_t.tile([P, 2, 2, P], F32, tag="bank")
-            for g in range(n):
+            flipped = pool.tile([P, 2, 2, P], F32, tag="bank")
+            for g in range(2):
                 for u in range(2):
                     nc.tensor.transpose(
                         out=flipped[:, g, u, :], in_=words[:, g, u * P : (u + 1) * P], identity=ident_f32[:]
                     )
             return flipped
 
-        def regroup_words(flipped, n):
-            grouped = work.tile([P, 2, P, PACK], BF16, align_bytes=64)
-            nc.scalar.copy(
-                out=grouped[:, 0:n].bitcast(F32), in_=flipped[:, 0:n].rearrange("p g u c -> p g c u")
-            )
-            return grouped
+        def regroup_words(copy, flipped, grouped):
+            copy(out=grouped.bitcast(F32), in_=flipped[:].rearrange("p g u c -> p g c u"))
 
-        def quantise_words(grouped, n, codes, scales):
+        def quantise(grouped, codes, scales):
             nc.vector.quantize_mx(
                 out=codes.rearrange("p g c -> p (g c)").bitcast(FP8X4),
                 scales=scales.rearrange("p g c -> p (g c)"),
-                in_=grouped[:, 0:n].rearrange("p g c t -> p (g c t)"),
+                in_=grouped.rearrange("p g c t -> p (g c t)"),
             )
 
         qkT = [keep.tile([P, H, 2, W], BF16, name="qkT%d" % w) for w in range(NW)]
@@ -81,51 +89,47 @@ def tile_hybridattention_pa_t_kernel(tc, x, Wv, q, k, out):
         q_raw = {}
         k_raw = {}
         x_raw = {}
-        in_psum = {}
-        in_sbuf = {}
+        x_grouped = {}
+        v_grouped = {}
 
-        def load_qk(w):
+        def load_qk(w, heads):
             rows = slice(w * W, (w + 1) * W)
-            q_raw[w] = raw.tile([P, H, TILES * HD], BF16, name="q_raw")
-            nc.sync.dma_start(
-                out=q_raw[w][:], in_=q[0, :, rows, :].rearrange("h (p j) d -> p h (j d)", j=TILES)
-            )
-            k_raw[w] = raw.tile([P, H, TILES * HD], BF16, name="k_raw")
-            for h in range(H):
+            if w not in q_raw:
+                q_raw[w] = raw.tile([P, H, TILES * HD], BF16, name="q_raw")
+                k_raw[w] = raw.tile([P, H, TILES * HD], BF16, name="k_raw")
+            for h in heads:
+                nc.sync.dma_start(
+                    out=q_raw[w][:, h, :], in_=q[0, h, rows, :].rearrange("(p j) d -> p (j d)", j=TILES)
+                )
                 nc.sync.dma_start(
                     out=k_raw[w][:, h, :].rearrange("p (j d) -> p j d", d=HD),
                     in_=k[0, h, rows, :].rearrange("(j p) d -> p j d", p=P),
                 )
 
         def load_x(w):
-            x_raw[w] = raw.tile([P, TILES, D], BF16, name="x_raw")
+            x_raw[w] = raw_x.tile([P, TILES, D], BF16, name="x_raw")
             nc.sync.dma_start(
                 out=x_raw[w][:].rearrange("p (u e) f -> p u (e f)", e=2),
                 in_=x[0, w * W : (w + 1) * W, :].rearrange("(u p e) f -> p u (e f)", u=2, e=2),
             )
 
-        def turn_qk(w, h):
-            turned = psum_t.tile([P, 2, W], BF16, tag="bank")
+        def turn_qk(w, h, pool=psum_t):
+            turned = pool.tile([P, 2, W], BF16, tag="bank")
             for i, src in enumerate((q_raw[w], k_raw[w])):
                 for j in range(TILES):
                     cols = slice(j * P, (j + 1) * P)
                     nc.tensor.transpose(out=turned[:, i, cols], in_=src[:, h, cols], identity=ident_bf16[:])
-            in_psum["qk"] = turned
+            return lambda: nc.vector.tensor_copy(out=qkT[w][:, h], in_=turned[:])
 
-        def keep_qk(w, h):
-            nc.vector.tensor_copy(out=qkT[w][:, h], in_=in_psum["qk"][:])
+        def flip_x(w, pair):
+            tiles = slice(2 * pair, 2 * pair + 2)
+            flipped = flip_words(psum_t, x_raw[w][:, tiles, :])
+            if pair == 0:
+                x_grouped[w] = prep.tile([P, TILES, P, PACK], BF16, name="x_grouped", align_bytes=64)
+            return lambda: regroup_words(nc.vector.tensor_copy, flipped, x_grouped[w][:, tiles])
 
-        def flip_x(w, t):
-            in_psum["x"] = flip_words(x_raw[w][:, t : t + 1, :], 1)
-
-        def regroup_x():
-            in_sbuf["x"] = regroup_words(in_psum["x"], 1)
-
-        def quantise_x(w, t):
-            quantise_words(in_sbuf["x"], 1, x_codes[w][:, t : t + 1, :], x_scales[w][:, t : t + 1, :])
-
-        def project_v(w, h):
-            v_ps = psum_t.tile([P, PACK, HD], F32, tag="bank")
+        def project_v(w, h, pool=psum_t):
+            v_ps = pool.tile([P, PACK, HD], F32, tag="bank")
             for t in range(PACK):
                 nc.tensor.matmul_mx(
                     out=v_ps[:, t, :],
@@ -136,25 +140,21 @@ def tile_hybridattention_pa_t_kernel(tc, x, Wv, q, k, out):
                     start=True,
                     stop=True,
                 )
-            in_psum["v"] = v_ps
+            if h == 0:
+                v_grouped[w] = prep.tile([P, H, HD, PACK], BF16, name="v_grouped", align_bytes=64)
+            return lambda: nc.scalar.copy(out=v_grouped[w][:, h], in_=v_ps[:].rearrange("p t d -> p d t"))
 
-        def round_v():
-            v_grouped = work.tile([P, HD, PACK], BF16, align_bytes=64)
-            nc.scalar.copy(out=v_grouped[:], in_=in_psum["v"][:].rearrange("p t d -> p d t"))
-            in_sbuf["v"] = v_grouped
+        def quantise_x(w):
+            quantise(x_grouped[w][:], x_codes[w][:], x_scales[w][:])
 
-        def quantise_v(w, h):
-            nc.vector.quantize_mx(
-                out=v_codes[w][:, h, :].bitcast(FP8X4),
-                scales=v_scales[w][:, h, :],
-                in_=in_sbuf["v"][:].rearrange("p d t -> p (d t)"),
-            )
+        def quantise_v(w):
+            quantise(v_grouped[w][:], v_codes[w][:], v_scales[w][:])
 
-        def where(n):
-            return n // (TILES * H), (n // H) % TILES, n % H
-
-        def key_windows(w):
-            return (0,) if w == 0 else (0, w)
+        def banks_of(n):
+            if n < ROUNDS_0:
+                return [(0, (BANKS * n) // H, (BANKS * n) % H + i, 0) for i in range(BANKS)]
+            w, tile = (n - ROUNDS_0) // ROUNDS + 1, (n - ROUNDS_0) % ROUNDS
+            return [(w, tile // H, tile % H, kw) for kw in (0, w)]
 
         s_ps = {}
         row_max = {}
@@ -166,93 +166,97 @@ def tile_hybridattention_pa_t_kernel(tc, x, Wv, q, k, out):
         e_codes = {}
         e_scales = {}
         o_ps = {}
-        total = {}
         inverse = {}
 
-        def scores(n):
-            w, j, h = where(n)
-            s_ps[n] = []
-            for kw in key_windows(w):
-                bank = psum_s.tile([P, W], F32)
-                nc.tensor.matmul(
-                    out=bank[:],
-                    lhsT=qkT[w][:, h, 0, j * P : (j + 1) * P],
-                    rhs=qkT[kw][:, h, 1, :],
-                    start=True,
-                    stop=True,
-                )
-                s_ps[n].append(bank)
+        def score(n, i):
+            w, j, h, kw = banks_of(n)[i]
+            s_ps[n, i] = psum_s.tile([P, W], F32, name="s_ps", tag="bank")
+            nc.tensor.matmul(
+                out=s_ps[n, i][:],
+                lhsT=qkT[w][:, h, 0, j * P : (j + 1) * P],
+                rhs=qkT[kw][:, h, 1, :],
+                start=True,
+                stop=True,
+            )
 
-        def row_maxima(n):
-            row_max[n] = small.tile([P, 2], F32, name="row_max")
-            for i, bank in enumerate(s_ps[n]):
-                nc.vector.tensor_reduce(out=row_max[n][:, i : i + 1], in_=bank[:], axis=AXIS_X, op=MAX)
+        def row_maximum(n, i):
+            if i == 0:
+                row_max[n] = small.tile([P, BANKS], F32, name="row_max")
+            nc.vector.tensor_reduce(out=row_max[n][:, i : i + 1], in_=s_ps[n, i][:], axis=AXIS_X, op=MAX)
 
         def exp_bias(n):
-            last = len(s_ps[n]) - 1
+            if n < ROUNDS_0:
+                bias[n] = small.tile([P, BANKS], F32, name="bias")
+                nc.gpsimd.tensor_scalar(
+                    out=bias[n][:], in0=row_max[n][:], scalar1=-SCALE, scalar2=None, op0=MULT
+                )
+                return
             bias[n] = small.tile([P, 1], F32, name="bias")
             nc.gpsimd.tensor_scalar(
                 out=bias[n][:],
                 in0=row_max[n][:, 0:1],
-                scalar1=row_max[n][:, last : last + 1],
+                scalar1=row_max[n][:, 1:2],
                 scalar2=-SCALE,
                 op0=MAX,
                 op1=MULT,
             )
 
-        def exponentials(n):
-            w, j, h = where(n)
-            if h == 0:
-                sums[w, j] = small.tile([P, H, 2], F32, name="sums")
-            e[n] = work.tile([P, 2, W], BF16, name="e")
-            for i, bank in enumerate(s_ps[n]):
-                nc.scalar.activation(
-                    out=e[n][:, i, :],
-                    in_=bank[:],
-                    func=EXP,
-                    bias=bias[n][:],
-                    scale=SCALE,
-                    accum_out=sums[w, j][:, h, i : i + 1],
-                )
+        def exponential(n, i):
+            w, j, h, kw = banks_of(n)[i]
+            if i == 0:
+                e[n] = work.tile([P, BANKS, W], BF16, name="e")
+                if h == 0:
+                    sums[w, j] = small.tile([P, BANKS, H], F32, name="sums")
+            source = 0 if w == 0 else i
+            column = i if w == 0 else 0
+            nc.scalar.activation(
+                out=e[n][:, i, :],
+                in_=s_ps[n, i][:],
+                func=EXP,
+                bias=bias[n][:, column : column + 1],
+                scale=SCALE,
+                accum_out=sums[w, j][:, source, h : h + 1],
+            )
 
         def flip_e(n):
-            n_kw = len(s_ps[n])
-            e_flipped[n] = flip_words(e[n][:, 0:n_kw, :], n_kw)
+            e_flipped[n] = flip_words(psum_e, e[n][:])
 
         def regroup_e(n):
-            e_grouped[n] = regroup_words(e_flipped[n], len(s_ps[n]))
+            half = n % 2
+            if half == 0:
+                e_grouped[n] = work.tile([P, 2 * BANKS, P, PACK], BF16, name="e_grouped", align_bytes=64)
+            slots = slice(half * BANKS, (half + 1) * BANKS)
+            regroup_words(nc.scalar.copy, e_flipped[n], e_grouped[n - half][:, slots])
 
         def quantise_e(n):
-            n_kw = len(s_ps[n])
-            e_codes[n] = work.tile([P, 2, P], U32, name="e_codes", align_bytes=64)
-            e_scales[n] = work.tile([P, 2, P], U8, name="e_scales", align_bytes=64)
-            quantise_words(e_grouped[n], n_kw, e_codes[n][:, 0:n_kw, :], e_scales[n][:, 0:n_kw, :])
+            e_codes[n] = work.tile([P, 2 * BANKS, P], U32, name="e_codes", align_bytes=64)
+            e_scales[n] = work.tile([P, 2 * BANKS, P], U8, name="e_scales", align_bytes=64)
+            quantise(e_grouped[n][:], e_codes[n][:], e_scales[n][:])
 
         def weigh_values(n):
-            w, j, h = where(n)
-            if h == 0:
-                o_ps[w, j] = psum_o.tile([P, H, HD], F32, name="o_ps")
-            windows = key_windows(w)
-            for i, kw in enumerate(windows):
+            half = n % 2
+            for i, (w, j, h, kw) in enumerate(banks_of(n)):
+                if h == 0 and kw == 0:
+                    o_ps[w, j] = psum_o.tile([P, H, HD], F32, name="o_ps", tag="bank")
+                slot = half * BANKS + i
                 nc.tensor.matmul_mx(
                     out=o_ps[w, j][:, h, :],
-                    lhsT=e_codes[n][:, i, :].bitcast(FP8X4),
-                    lhsT_scale=e_scales[n][:, i, :],
+                    lhsT=e_codes[n - half][:, slot, :].bitcast(FP8X4),
+                    lhsT_scale=e_scales[n - half][:, slot, :],
                     rhs=v_codes[kw][:, h, :].bitcast(FP8X4),
                     rhs_scale=v_scales[kw][:, h, :],
-                    start=(i == 0),
-                    stop=(i == len(windows) - 1),
+                    start=(kw == 0),
+                    stop=(kw == w),
                 )
-
-        def add_sums(w, j):
-            total[w, j] = small.tile([P, H], F32, name="total")
-            nc.gpsimd.tensor_tensor(
-                out=total[w, j][:], in0=sums[w, j][:, :, 0], in1=sums[w, j][:, :, 1], op=ADD
-            )
 
         def invert_sums(w, j):
             inverse[w, j] = small.tile([P, H], F32, name="inverse")
-            nc.vector.reciprocal(out=inverse[w, j][:], in_=sums[w, j][:, :, 0] if w == 0 else total[w, j][:])
+            total = sums[w, j][:, 0]
+            if w > 0:
+                both = small.tile([P, H], F32)
+                nc.gpsimd.tensor_tensor(out=both[:], in0=total, in1=sums[w, j][:, 1], op=ADD)
+                total = both[:]
+            nc.gpsimd.tensor_tensor(out=inverse[w, j][:], in0=total, in1=minus_one[:], op=POW)
 
         def divide_and_store(w, j):
             o_sb = work.tile([P, H, HD], F32)
@@ -268,70 +272,130 @@ def tile_hybridattention_pa_t_kernel(tc, x, Wv, q, k, out):
             )
 
         wv_raw = const.tile([P, TILES, D], BF16)
+        load_qk(0, range(1))
         load_x(0)
+        load_qk(0, range(1, 2))
         nc.sync.dma_start(out=wv_raw[:], in_=Wv.rearrange("(o p) f -> p o f", p=P))
+        load_qk(0, range(2, H))
+        load_x(1)
+        load_qk(1, range(H))
         wv_codes = const.tile([P, TILES, P], U32, align_bytes=64)
         wv_scales = const.tile([P, TILES, P], U8, align_bytes=64)
-        for o in range(0, TILES, 2):
-            wv_grouped = regroup_words(flip_words(wv_raw[:, o : o + 2, :], 2), 2)
-            quantise_words(wv_grouped, 2, wv_codes[:, o : o + 2, :], wv_scales[:, o : o + 2, :])
+        x_grouped[0] = prep.tile([P, TILES, P, PACK], BF16, name="x_grouped", align_bytes=64)
+        wv_grouped = prep.tile([P, TILES, P, PACK], BF16, name="v_grouped", align_bytes=64)
 
-        def if_tile(stage, n):
-            if 0 <= n < N_TILES:
-                stage(n)
+        halves = (slice(0, 2), slice(2, 4))
 
-        def chain_started(n, first_round, ahead):
-            w, j, h = where(n)
-            return (w + ahead, j) if h == first_round and 0 <= w + ahead < NW else None
+        turn_qk(0, 0)()
+        flips = [flip_words(psum_s, x_raw[0][:, t, :]) for t in halves]
+        score(0, 0)
+        keep_qk = turn_qk(0, 1, psum_e)
+        flips += [flip_words(psum_s, wv_raw[:, t, :]) for t in halves]
+        row_maximum(0, 0)
+        for half, t in enumerate(halves):
+            regroup_words(nc.scalar.copy, flips[half], x_grouped[0][:, t])
+            quantise(x_grouped[0][:, t], x_codes[0][:, t], x_scales[0][:, t])
+        keep_qk()
+        score(0, 1)
+        for half, t in enumerate(halves):
+            regroup_words(nc.scalar.copy, flips[2 + half], wv_grouped[:, t])
+            if half == 0:
+                row_maximum(0, 1)
+                exp_bias(0)
+            quantise(wv_grouped[:, t], wv_codes[:, t], wv_scales[:, t])
+        keep_qk = turn_qk(0, 2, psum_e)
+        copies = [project_v(0, 0), project_v(0, 1, psum_o)]
+        exponential(0, 0)
+        exponential(0, 1)
+        keep_qk()
+        score(1, 0)
+        row_maximum(1, 0)
+        keep_qk = turn_qk(0, 3, psum_e)
+        copies[0]()
+        copies[1]()
+        keep_qk()
+        score(1, 1)
+        row_maximum(1, 1)
+        exp_bias(1)
+        score(2, 0)
+        copies = [project_v(0, 2), project_v(0, 3, psum_o)]
+        copies[0]()
+        copies[1]()
+        quantise_v(0)
 
-        def x_tile(n):
-            return chain_started(n, 0, 2)
+        chains = {}
+        quantises = {}
 
-        def v_head(n):
-            return chain_started(n, 2, 1)
+        def plan(chain, w, i, wanted):
+            n = wanted
+            while n in chains:
+                n += 1
+            chains[n] = (chain, w, i)
+            return n
 
-        def qk_head(n):
-            return chain_started(n, 3, 1)
+        for w in range(1, NW):
+            for h in range(H):
+                plan(turn_qk, w, h, max(first_round(w) - ROUNDS, H) + 4 * h if w > 1 else H + h)
+        for w in range(1, NW):
+            begin = first_round(w)
+            n = plan(flip_x, w, 0, max(begin - 27, 0))
+            n = plan(flip_x, w, 1, max(begin - 23, n + 1))
+            quantises[max(begin - 19, n)] = (quantise_x, w)
+            n = max(begin - 19, n)
+            for h in range(H):
+                n = plan(project_v, w, h, max(begin - 13 + 4 * h, n + 1))
+            quantises[n + 1 if w == 1 else n + 2] = (quantise_v, w)
 
-        for n in range(-2 * TILES * H, N_TILES + 4):
-            w, j, h = where(n)
-            if h == 0 and j == 0:
-                if w + 2 < NW:
-                    load_qk(w + 2)
-                if w + 3 < NW:
-                    load_x(w + 3)
+        def has(n):
+            return 0 <= n < N_ROUNDS
 
-            if_tile(scores, n + 1)
-            if_tile(flip_e, n - 1)
+        for n in range(0, N_ROUNDS + 5):
+            for w in range(2, NW):
+                if n == max(first_round(w) - 32, 0):
+                    load_x(w)
+                if n == first_round(w) - 24:
+                    load_qk(w, range(H))
 
-            finished = where(n - H)[0:2] if h == H - 1 and n - H >= 0 else None
-            if_tile(row_maxima, n)
-            if finished:
-                invert_sums(*finished)
-            if_tile(quantise_e, n - 3)
-            if_tile(exp_bias, n)
-            if qk_head(n - 1):
-                keep_qk(*qk_head(n - 1))
-            if finished:
-                divide_and_store(*finished)
-            if x_tile(n - 3):
-                quantise_x(*x_tile(n - 3))
-            if v_head(n - 3):
-                quantise_v(*v_head(n - 3))
+            if has(n - 1):
+                flip_e(n - 1)
+            copy = None
+            if n in chains:
+                chain, for_w, i = chains[n]
+                copy = chain(for_w, i)
+            if n % 2 == 0 and has(n - 4):
+                weigh_values(n - 4)
+                weigh_values(n - 3)
+            if has(n) and n > 0:
+                exponential(n, 0)
+            if has(n + 2):
+                score(n + 2, 1)
+            if has(n) and n > 0:
+                exponential(n, 1)
+            if has(n + 3):
+                score(n + 3, 0)
 
-            if_tile(exponentials, n)
-            if_tile(regroup_e, n - 1)
-            if x_tile(n - 1):
-                regroup_x()
-            if v_head(n - 1):
-                round_v()
-            if h == H - 1 and 0 < w < NW:
-                add_sums(w, j)
+            if has(n + 2):
+                row_maximum(n + 2, 0)
+            if n % 2 == 1 and has(n - 3):
+                quantise_e(n - 3)
+            if copy and chain != project_v:
+                copy()
+            if has(n + 2):
+                row_maximum(n + 2, 1)
+                exp_bias(n + 2)
+            if n % 2 == 0 and has(n - 4):
+                w, j, h, kw = banks_of(n - 3)[1]
+                if h == H - 1:
+                    divide_and_store(w, j)
+            if n in quantises:
+                step, for_w = quantises[n]
+                step(for_w)
 
-            if_tile(weigh_values, n - 3)
-            if v_head(n):
-                project_v(*v_head(n))
-            if x_tile(n):
-                flip_x(*x_tile(n))
-            if qk_head(n):
-                turn_qk(*qk_head(n))
+            if has(n - 1):
+                regroup_e(n - 1)
+            if copy and chain == project_v:
+                copy()
+            if has(n):
+                w, j, h, kw = banks_of(n)[1]
+                if h == H - 1:
+                    invert_sums(w, j)

@@ -12,7 +12,6 @@ EXP = mybir.ActivationFunctionType.Exp
 MAX = mybir.AluOpType.max
 MULT = mybir.AluOpType.mult
 ADD = mybir.AluOpType.add
-POW = mybir.AluOpType.pow
 AXIS_X = mybir.AxisListType.X
 
 P = 128
@@ -58,8 +57,6 @@ def tile_hybridattention_pa_t_kernel(tc, x, Wv, q, k, out):
         make_identity(nc, ident_bf16[:])
         ident_f32 = const.tile([P, P], F32)
         make_identity(nc, ident_f32[:])
-        minus_one = const.tile([P, H], F32)
-        nc.gpsimd.memset(minus_one[:], -1.0)
 
         def flip_words(pool, rows):
             words = rows.bitcast(F32)
@@ -166,6 +163,7 @@ def tile_hybridattention_pa_t_kernel(tc, x, Wv, q, k, out):
         e_codes = {}
         e_scales = {}
         o_ps = {}
+        total = {}
         inverse = {}
 
         def score(n, i):
@@ -249,14 +247,16 @@ def tile_hybridattention_pa_t_kernel(tc, x, Wv, q, k, out):
                     stop=(kw == w),
                 )
 
+        def add_sums(w, j):
+            if w > 0:
+                total[w, j] = small.tile([P, H], F32, name="total")
+                nc.gpsimd.tensor_tensor(
+                    out=total[w, j][:], in0=sums[w, j][:, 0], in1=sums[w, j][:, 1], op=ADD
+                )
+
         def invert_sums(w, j):
             inverse[w, j] = small.tile([P, H], F32, name="inverse")
-            total = sums[w, j][:, 0]
-            if w > 0:
-                both = small.tile([P, H], F32)
-                nc.gpsimd.tensor_tensor(out=both[:], in0=total, in1=sums[w, j][:, 1], op=ADD)
-                total = both[:]
-            nc.gpsimd.tensor_tensor(out=inverse[w, j][:], in0=total, in1=minus_one[:], op=POW)
+            nc.vector.reciprocal(out=inverse[w, j][:], in_=sums[w, j][:, 0] if w == 0 else total[w, j][:])
 
         def divide_and_store(w, j):
             o_sb = work.tile([P, H, HD], F32)
@@ -374,6 +374,12 @@ def tile_hybridattention_pa_t_kernel(tc, x, Wv, q, k, out):
             if has(n + 3):
                 score(n + 3, 0)
 
+            finished = None
+            if n % 2 == 0 and has(n - 4):
+                w, j, h, kw = banks_of(n - 3)[1]
+                if h == H - 1:
+                    finished = w, j
+                    invert_sums(w, j)
             if has(n + 2):
                 row_maximum(n + 2, 0)
             if n % 2 == 1 and has(n - 3):
@@ -383,10 +389,8 @@ def tile_hybridattention_pa_t_kernel(tc, x, Wv, q, k, out):
             if has(n + 2):
                 row_maximum(n + 2, 1)
                 exp_bias(n + 2)
-            if n % 2 == 0 and has(n - 4):
-                w, j, h, kw = banks_of(n - 3)[1]
-                if h == H - 1:
-                    divide_and_store(w, j)
+            if finished:
+                divide_and_store(*finished)
             if n in quantises:
                 step, for_w = quantises[n]
                 step(for_w)
@@ -398,4 +402,4 @@ def tile_hybridattention_pa_t_kernel(tc, x, Wv, q, k, out):
             if has(n):
                 w, j, h, kw = banks_of(n)[1]
                 if h == H - 1:
-                    invert_sums(w, j)
+                    add_sums(w, j)

@@ -116,14 +116,16 @@ def tile_hybridattention_pa_t_kernel(tc, x, Wv, q, k, out):
                 for j in range(TILES):
                     cols = slice(j * P, (j + 1) * P)
                     nc.tensor.transpose(out=turned[:, i, cols], in_=src[:, h, cols], identity=ident_bf16[:])
-            return lambda: nc.vector.tensor_copy(out=qkT[w][:, h], in_=turned[:])
+            return False, lambda: nc.vector.tensor_copy(out=qkT[w][:, h], in_=turned[:])
 
         def flip_x(w, pair):
             tiles = slice(2 * pair, 2 * pair + 2)
             flipped = flip_words(psum_t, x_raw[w][:, tiles, :])
             if pair == 0:
                 x_grouped[w] = prep.tile([P, TILES, P, PACK], BF16, name="x_grouped", align_bytes=64)
-            return lambda: regroup_words(nc.vector.tensor_copy, flipped, x_grouped[w][:, tiles])
+            on_scalar = w <= 2
+            copy = nc.scalar.copy if on_scalar else nc.vector.tensor_copy
+            return on_scalar, lambda: regroup_words(copy, flipped, x_grouped[w][:, tiles])
 
         def project_v(w, h, pool=psum_t):
             v_ps = pool.tile([P, PACK, HD], F32, tag="bank")
@@ -139,7 +141,7 @@ def tile_hybridattention_pa_t_kernel(tc, x, Wv, q, k, out):
                 )
             if h == 0:
                 v_grouped[w] = prep.tile([P, H, HD, PACK], BF16, name="v_grouped", align_bytes=64)
-            return lambda: nc.scalar.copy(out=v_grouped[w][:, h], in_=v_ps[:].rearrange("p t d -> p d t"))
+            return True, lambda: nc.scalar.copy(out=v_grouped[w][:, h], in_=v_ps[:].rearrange("p t d -> p d t"))
 
         def quantise_x(w):
             quantise(x_grouped[w][:], x_codes[w][:], x_scales[w][:])
@@ -272,55 +274,49 @@ def tile_hybridattention_pa_t_kernel(tc, x, Wv, q, k, out):
             )
 
         wv_raw = const.tile([P, TILES, D], BF16)
-        load_qk(0, range(1))
+        load_qk(0, range(BANKS))
         load_x(0)
-        load_qk(0, range(1, 2))
         nc.sync.dma_start(out=wv_raw[:], in_=Wv.rearrange("(o p) f -> p o f", p=P))
-        load_qk(0, range(2, H))
+        load_qk(0, range(BANKS, H))
         load_x(1)
         load_qk(1, range(H))
         wv_codes = const.tile([P, TILES, P], U32, align_bytes=64)
         wv_scales = const.tile([P, TILES, P], U8, align_bytes=64)
         x_grouped[0] = prep.tile([P, TILES, P, PACK], BF16, name="x_grouped", align_bytes=64)
         wv_grouped = prep.tile([P, TILES, P, PACK], BF16, name="v_grouped", align_bytes=64)
-
-        halves = (slice(0, 2), slice(2, 4))
-
-        turn_qk(0, 0)()
-        flips = [flip_words(psum_s, x_raw[0][:, t, :]) for t in halves]
-        score(0, 0)
-        keep_qk = turn_qk(0, 1, psum_e)
-        flips += [flip_words(psum_s, wv_raw[:, t, :]) for t in halves]
-        row_maximum(0, 0)
-        for half, t in enumerate(halves):
-            regroup_words(nc.scalar.copy, flips[half], x_grouped[0][:, t])
-            quantise(x_grouped[0][:, t], x_codes[0][:, t], x_scales[0][:, t])
-        keep_qk()
-        score(0, 1)
-        for half, t in enumerate(halves):
-            regroup_words(nc.scalar.copy, flips[2 + half], wv_grouped[:, t])
-            if half == 0:
-                row_maximum(0, 1)
+        turn_qk(0, 0)[1]()
+        turn_qk(0, 1, psum_e)[1]()
+        for rows, grouped, codes, scales in (
+            (x_raw[0], x_grouped[0], x_codes[0], x_scales[0]),
+            (wv_raw, wv_grouped, wv_codes, wv_scales),
+        ):
+            halves = (slice(0, 2), slice(2, 4))
+            flips = [flip_words(psum_s, rows[:, t, :]) for t in halves]
+            if rows is wv_raw:
+                keeps = [turn_qk(0, 2), turn_qk(0, 3, psum_e)]
+            else:
+                for i in range(BANKS):
+                    score(0, i)
+                    row_maximum(0, i)
                 exp_bias(0)
-            quantise(wv_grouped[:, t], wv_codes[:, t], wv_scales[:, t])
-        keep_qk = turn_qk(0, 2, psum_e)
-        copies = [project_v(0, 0), project_v(0, 1, psum_o)]
-        exponential(0, 0)
-        exponential(0, 1)
-        keep_qk()
-        score(1, 0)
-        row_maximum(1, 0)
-        keep_qk = turn_qk(0, 3, psum_e)
-        copies[0]()
-        copies[1]()
-        keep_qk()
-        score(1, 1)
-        row_maximum(1, 1)
+            for flipped, t in zip(flips, halves):
+                regroup_words(nc.scalar.copy, flipped, grouped[:, t])
+                quantise(grouped[:, t], codes[:, t], scales[:, t])
+        copies = [project_v(0, 0, psum_o)]
+        for on_scalar, keep_qk in keeps:
+            keep_qk()
+        for i in range(BANKS):
+            exponential(0, i)
+        copies += [project_v(0, 1), project_v(0, 2, psum_e)]
+        for i in range(BANKS):
+            score(1, i)
+            row_maximum(1, i)
         exp_bias(1)
         score(2, 0)
-        copies = [project_v(0, 2), project_v(0, 3, psum_o)]
-        copies[0]()
-        copies[1]()
+        copies[0][1]()
+        copies.append(project_v(0, 3, psum_o))
+        for on_scalar, copy_v in copies[1:]:
+            copy_v()
         quantise_v(0)
 
         chains = {}
@@ -361,7 +357,7 @@ def tile_hybridattention_pa_t_kernel(tc, x, Wv, q, k, out):
             copy = None
             if n in chains:
                 chain, for_w, i = chains[n]
-                copy = chain(for_w, i)
+                on_scalar, copy = chain(for_w, i)
             if n % 2 == 0 and has(n - 4):
                 weigh_values(n - 4)
                 weigh_values(n - 3)
@@ -384,22 +380,23 @@ def tile_hybridattention_pa_t_kernel(tc, x, Wv, q, k, out):
                 row_maximum(n + 2, 0)
             if n % 2 == 1 and has(n - 3):
                 quantise_e(n - 3)
-            if copy and chain != project_v:
+            if copy and not on_scalar:
                 copy()
             if has(n + 2):
                 row_maximum(n + 2, 1)
                 exp_bias(n + 2)
             if finished:
                 divide_and_store(*finished)
-            if n in quantises:
-                step, for_w = quantises[n]
-                step(for_w)
 
             if has(n - 1):
                 regroup_e(n - 1)
-            if copy and chain == project_v:
+            if copy and on_scalar:
                 copy()
             if has(n):
                 w, j, h, kw = banks_of(n)[1]
                 if h == H - 1:
                     add_sums(w, j)
+
+            if n in quantises:
+                step, for_w = quantises[n]
+                step(for_w)

@@ -105,10 +105,12 @@ def tile_hybridattention_pa_t_kernel(tc, x, Wv, q, k, out):
 
         def load_x(w):
             x_raw[w] = raw_x.tile([P, TILES, D], BF16, name="x_raw")
-            nc.sync.dma_start(
-                out=x_raw[w][:].rearrange("p (u e) f -> p u (e f)", e=2),
-                in_=x[0, w * W : (w + 1) * W, :].rearrange("(u p e) f -> p u (e f)", u=2, e=2),
-            )
+            for u in range(2):
+                first = w * W + u * 2 * P
+                nc.sync.dma_start(
+                    out=x_raw[w][:, 2 * u : 2 * u + 2, :].rearrange("p e f -> p (e f)"),
+                    in_=x[0, first : first + 2 * P, :].rearrange("(p e) f -> p (e f)", e=2),
+                )
 
         def turn_qk(w, h, pool=psum_t):
             turned = pool.tile([P, 2, W], BF16, tag="bank")
@@ -276,7 +278,11 @@ def tile_hybridattention_pa_t_kernel(tc, x, Wv, q, k, out):
         wv_raw = const.tile([P, TILES, D], BF16)
         load_qk(0, range(BANKS))
         load_x(0)
-        nc.sync.dma_start(out=wv_raw[:], in_=Wv.rearrange("(o p) f -> p o f", p=P))
+        for half in range(2):
+            nc.sync.dma_start(
+                out=wv_raw[:, 2 * half : 2 * half + 2, :],
+                in_=Wv[2 * half * P : 2 * (half + 1) * P, :].rearrange("(o p) f -> p o f", p=P),
+            )
         load_qk(0, range(BANKS, H))
         load_x(1)
         load_qk(1, range(H))
@@ -358,13 +364,13 @@ def tile_hybridattention_pa_t_kernel(tc, x, Wv, q, k, out):
             if n in chains:
                 chain, for_w, i = chains[n]
                 on_scalar, copy = chain(for_w, i)
-            if n % 2 == 0 and has(n - 4):
-                weigh_values(n - 4)
-                weigh_values(n - 3)
             if has(n) and n > 0:
                 exponential(n, 0)
             if has(n + 2):
                 score(n + 2, 1)
+            if n % 2 == 0 and has(n - 4):
+                weigh_values(n - 4)
+                weigh_values(n - 3)
             if has(n) and n > 0:
                 exponential(n, 1)
             if has(n + 3):

@@ -224,27 +224,22 @@ def tile_hybridattention_pa_t_kernel(tc, x, Wv, q, k, out):
             e_flipped[n] = flip_words(psum_e, e[n][:])
 
         def regroup_e(n):
-            half = n % 2
-            if half == 0:
-                e_grouped[n] = work.tile([P, 2 * BANKS, P, PACK], BF16, name="e_grouped", align_bytes=64)
-            slots = slice(half * BANKS, (half + 1) * BANKS)
-            regroup_words(nc.scalar.copy, e_flipped[n], e_grouped[n - half][:, slots])
+            e_grouped[n] = work.tile([P, BANKS, P, PACK], BF16, name="e_grouped", align_bytes=64)
+            regroup_words(nc.scalar.copy, e_flipped[n], e_grouped[n][:])
 
         def quantise_e(n):
-            e_codes[n] = work.tile([P, 2 * BANKS, P], U32, name="e_codes", align_bytes=64)
-            e_scales[n] = work.tile([P, 2 * BANKS, P], U8, name="e_scales", align_bytes=64)
+            e_codes[n] = work.tile([P, BANKS, P], U32, name="e_codes", align_bytes=64)
+            e_scales[n] = work.tile([P, BANKS, P], U8, name="e_scales", align_bytes=64)
             quantise(e_grouped[n][:], e_codes[n][:], e_scales[n][:])
 
         def weigh_values(n):
-            half = n % 2
             for i, (w, j, h, kw) in enumerate(banks_of(n)):
                 if h == 0 and kw == 0:
                     o_ps[w, j] = psum_o.tile([P, H, HD], F32, name="o_ps", tag="bank")
-                slot = half * BANKS + i
                 nc.tensor.matmul_mx(
                     out=o_ps[w, j][:, h, :],
-                    lhsT=e_codes[n - half][:, slot, :].bitcast(FP8X4),
-                    lhsT_scale=e_scales[n - half][:, slot, :],
+                    lhsT=e_codes[n][:, i, :].bitcast(FP8X4),
+                    lhsT_scale=e_scales[n][:, i, :],
                     rhs=v_codes[kw][:, h, :].bitcast(FP8X4),
                     rhs_scale=v_scales[kw][:, h, :],
                     start=(kw == 0),
@@ -336,10 +331,9 @@ def tile_hybridattention_pa_t_kernel(tc, x, Wv, q, k, out):
             return n
 
         for w in range(1, NW):
-            for h in range(H):
-                plan(turn_qk, w, h, max(first_round(w) - ROUNDS, H) + 4 * h if w > 1 else H + h)
-        for w in range(1, NW):
             begin = first_round(w)
+            for h in range(H):
+                plan(turn_qk, w, h, begin - ROUNDS + 4 * h if w > 1 else 2 * h + 1)
             n = plan(flip_x, w, 0, max(begin - 27, 0))
             n = plan(flip_x, w, 1, max(begin - 23, n + 1))
             quantises[max(begin - 19, n)] = (quantise_x, w)
@@ -351,7 +345,7 @@ def tile_hybridattention_pa_t_kernel(tc, x, Wv, q, k, out):
         def has(n):
             return 0 <= n < N_ROUNDS
 
-        for n in range(0, N_ROUNDS + 5):
+        for n in range(0, N_ROUNDS + 3):
             for w in range(2, NW):
                 if n == max(first_round(w) - 32, 0):
                     load_x(w)
@@ -368,8 +362,7 @@ def tile_hybridattention_pa_t_kernel(tc, x, Wv, q, k, out):
                 exponential(n, 0)
             if has(n + 2):
                 score(n + 2, 1)
-            if n % 2 == 0 and has(n - 4):
-                weigh_values(n - 4)
+            if has(n - 3):
                 weigh_values(n - 3)
             if has(n) and n > 0:
                 exponential(n, 1)
@@ -377,15 +370,15 @@ def tile_hybridattention_pa_t_kernel(tc, x, Wv, q, k, out):
                 score(n + 3, 0)
 
             finished = None
-            if n % 2 == 0 and has(n - 4):
+            if has(n - 3):
                 w, j, h, kw = banks_of(n - 3)[1]
                 if h == H - 1:
                     finished = w, j
                     invert_sums(w, j)
             if has(n + 2):
                 row_maximum(n + 2, 0)
-            if n % 2 == 1 and has(n - 3):
-                quantise_e(n - 3)
+            if has(n - 2):
+                quantise_e(n - 2)
             if copy and not on_scalar:
                 copy()
             if has(n + 2):

@@ -59,9 +59,10 @@ def tile_hybridattention_pa_t_kernel(tc, x, Wv, q, k, out):
         make_identity(nc, ident_f32[:])
 
         def flip_words(pool, rows):
+            n = rows.shape[1]
             words = rows.bitcast(F32)
-            flipped = pool.tile([P, 2, 2, P], F32, tag="bank")
-            for g in range(2):
+            flipped = pool.tile([P, n, 2, P], F32, tag="bank")
+            for g in range(n):
                 for u in range(2):
                     nc.tensor.transpose(
                         out=flipped[:, g, u, :], in_=words[:, g, u * P : (u + 1) * P], identity=ident_f32[:]
@@ -342,6 +343,8 @@ def tile_hybridattention_pa_t_kernel(tc, x, Wv, q, k, out):
                 n = plan(project_v, w, h, max(begin - 13 + 4 * h, n + 1))
             quantises[n + 1 if w == 1 else n + 2] = (quantise_v, w)
 
+        LAST = N_ROUNDS - 1
+
         def has(n):
             return 0 <= n < N_ROUNDS
 
@@ -352,7 +355,7 @@ def tile_hybridattention_pa_t_kernel(tc, x, Wv, q, k, out):
                 if n == first_round(w) - 24:
                     load_qk(w, range(H))
 
-            if has(n - 1):
+            if has(n - 1) and n <= LAST:
                 flip_e(n - 1)
             copy = None
             if n in chains:
@@ -360,12 +363,16 @@ def tile_hybridattention_pa_t_kernel(tc, x, Wv, q, k, out):
                 on_scalar, copy = chain(for_w, i)
             if has(n) and n > 0:
                 exponential(n, 0)
+            if n == LAST:
+                end_flips = [flip_words(psum_s, e[n][:, 0:1])]
             if has(n + 2):
                 score(n + 2, 1)
             if has(n - 3):
                 weigh_values(n - 3)
             if has(n) and n > 0:
                 exponential(n, 1)
+            if n == LAST:
+                end_flips.append(flip_words(psum_s, e[n][:, 1:2]))
             if has(n + 3):
                 score(n + 3, 0)
 
@@ -374,11 +381,24 @@ def tile_hybridattention_pa_t_kernel(tc, x, Wv, q, k, out):
                 w, j, h, kw = banks_of(n - 3)[1]
                 if h == H - 1:
                     finished = w, j
-                    invert_sums(w, j)
+                    if n - 3 < LAST:
+                        invert_sums(w, j)
             if has(n + 2):
                 row_maximum(n + 2, 0)
-            if has(n - 2):
+            if n == LAST + 1:
+                e_grouped[LAST] = work.tile([P, BANKS, P, PACK], BF16, name="e_grouped", align_bytes=64)
+                e_codes[LAST] = work.tile([P, BANKS, P], U32, name="e_codes", align_bytes=64)
+                e_scales[LAST] = work.tile([P, BANKS, P], U8, name="e_scales", align_bytes=64)
+                regroup_words(nc.vector.tensor_copy, end_flips[0], e_grouped[LAST][:, 0:1])
+                w, j, h, kw = banks_of(LAST)[1]
+                invert_sums(w, j)
+            if has(n - 2) and n < LAST + 2:
                 quantise_e(n - 2)
+            if n == LAST + 1:
+                regroup_words(nc.scalar.copy, end_flips[1], e_grouped[LAST][:, 1:2])
+                for i in range(BANKS):
+                    t = slice(i, i + 1)
+                    quantise(e_grouped[LAST][:, t], e_codes[LAST][:, t], e_scales[LAST][:, t])
             if copy and not on_scalar:
                 copy()
             if has(n + 2):
@@ -387,7 +407,7 @@ def tile_hybridattention_pa_t_kernel(tc, x, Wv, q, k, out):
             if finished:
                 divide_and_store(*finished)
 
-            if has(n - 1):
+            if has(n - 1) and n <= LAST:
                 regroup_e(n - 1)
             if copy and on_scalar:
                 copy()

from contextlib import ExitStack

import concourse.mybir as mybir
from concourse.masks import make_identity

BF16 = mybir.dt.bfloat16
F32 = mybir.dt.float32
U32 = mybir.dt.uint32
U8 = mybir.dt.uint8
FP8X4 = mybir.dt.float8_e4m3fn_x4
EXP = mybir.ActivationFunctionType.Exp
MAX = mybir.AluOpType.max
MULT = mybir.AluOpType.mult
ADD = mybir.AluOpType.add
AXIS_X = mybir.AxisListType.X

P = 128
PACK = 4
T = 4096
H = 4
HD = 128
D = H * HD
W = 512
NW = T // W
TILES = W // P
SCALE = HD**-0.5

BANKS = 2
ROUNDS = TILES * H
ROUNDS_0 = ROUNDS // BANKS
N_ROUNDS = ROUNDS_0 + (NW - 1) * ROUNDS

FLOPS = 2 * T * D * D + 2 * (2 * H * T * (2 * W) * HD)


def first_round(w):
    return 0 if w == 0 else ROUNDS_0 + (w - 1) * ROUNDS


def tile_hybridattention_pa_t_kernel(tc, x, Wv, q, k, out):
    nc = tc.nc
    with ExitStack() as ctx:
        const = ctx.enter_context(tc.tile_pool(name="const", bufs=1))
        keep = ctx.enter_context(tc.tile_pool(name="keep", bufs=1))
        raw = ctx.enter_context(tc.tile_pool(name="raw", bufs=2))
        raw_x = ctx.enter_context(tc.tile_pool(name="raw_x", bufs=3))
        prep = ctx.enter_context(tc.tile_pool(name="prep", bufs=2))
        work = ctx.enter_context(tc.tile_pool(name="work", bufs=4))
        small = ctx.enter_context(tc.tile_pool(name="small", bufs=6))
        psum_s = ctx.enter_context(tc.psum_pool(name="psum_s", bufs=5))
        psum_e = ctx.enter_context(tc.psum_pool(name="psum_e", bufs=1))
        psum_t = ctx.enter_context(tc.psum_pool(name="psum_t", bufs=1))
        psum_o = ctx.enter_context(tc.psum_pool(name="psum_o", bufs=1))
        ctx.enter_context(tc.manual_schedule())

        ident_bf16 = const.tile([P, P], BF16)
        make_identity(nc, ident_bf16[:])
        ident_f32 = const.tile([P, P], F32)
        make_identity(nc, ident_f32[:])

        def flip_words(pool, rows):
            n = rows.shape[1]
            words = rows.bitcast(F32)
            flipped = pool.tile([P, n, 2, P], F32, tag="bank")
            for g in range(n):
                for u in range(2):
                    nc.tensor.transpose(
                        out=flipped[:, g, u, :], in_=words[:, g, u * P : (u + 1) * P], identity=ident_f32[:]
                    )
            return flipped

        def regroup_words(copy, flipped, grouped):
            copy(out=grouped.bitcast(F32), in_=flipped[:].rearrange("p g u c -> p g c u"))

        def quantise(grouped, codes, scales):
            nc.vector.quantize_mx(
                out=codes.rearrange("p g c -> p (g c)").bitcast(FP8X4),
                scales=scales.rearrange("p g c -> p (g c)"),
                in_=grouped.rearrange("p g c t -> p (g c t)"),
            )

        qkT = [keep.tile([P, H, 2, W], BF16, name="qkT%d" % w) for w in range(NW)]
        x_codes = [keep.tile([P, TILES, P], U32, name="x_codes%d" % w, align_bytes=64) for w in range(NW)]
        x_scales = [keep.tile([P, TILES, P], U8, name="x_scales%d" % w, align_bytes=64) for w in range(NW)]
        v_codes = [keep.tile([P, H, HD], U32, name="v_codes%d" % w, align_bytes=64) for w in range(NW)]
        v_scales = [keep.tile([P, H, HD], U8, name="v_scales%d" % w, align_bytes=64) for w in range(NW)]
        q_raw = {}
        k_raw = {}
        x_raw = {}
        x_grouped = {}
        v_grouped = {}

        def load_qk(w, heads):
            rows = slice(w * W, (w + 1) * W)
            if w not in q_raw:
                q_raw[w] = raw.tile([P, H, TILES * HD], BF16, name="q_raw")
                k_raw[w] = raw.tile([P, H, TILES * HD], BF16, name="k_raw")
            for h in heads:
                nc.sync.dma_start(
                    out=q_raw[w][:, h, :], in_=q[0, h, rows, :].rearrange("(p j) d -> p (j d)", j=TILES)
                )
                nc.sync.dma_start(
                    out=k_raw[w][:, h, :].rearrange("p (j d) -> p j d", d=HD),
                    in_=k[0, h, rows, :].rearrange("(j p) d -> p j d", p=P),
                )

        def load_x(w):
            x_raw[w] = raw_x.tile([P, TILES, D], BF16, name="x_raw")
            for u in range(2):
                first = w * W + u * 2 * P
                nc.sync.dma_start(
                    out=x_raw[w][:, 2 * u : 2 * u + 2, :].rearrange("p e f -> p (e f)"),
                    in_=x[0, first : first + 2 * P, :].rearrange("(p e) f -> p (e f)", e=2),
                )

        def turn_qk(w, h, pool=psum_t):
            turned = pool.tile([P, 2, W], BF16, tag="bank")
            for i, src in enumerate((q_raw[w], k_raw[w])):
                for j in range(TILES):
                    cols = slice(j * P, (j + 1) * P)
                    nc.tensor.transpose(out=turned[:, i, cols], in_=src[:, h, cols], identity=ident_bf16[:])
            return False, lambda: nc.vector.tensor_copy(out=qkT[w][:, h], in_=turned[:])

        def flip_x(w, pair):
            tiles = slice(2 * pair, 2 * pair + 2)
            flipped = flip_words(psum_t, x_raw[w][:, tiles, :])
            if pair == 0:
                x_grouped[w] = prep.tile([P, TILES, P, PACK], BF16, name="x_grouped", align_bytes=64)
            on_scalar = w <= 2
            copy = nc.scalar.copy if on_scalar else nc.vector.tensor_copy
            return on_scalar, lambda: regroup_words(copy, flipped, x_grouped[w][:, tiles])

        def project_v(w, h, pool=psum_t):
            v_ps = pool.tile([P, PACK, HD], F32, tag="bank")
            for t in range(PACK):
                nc.tensor.matmul_mx(
                    out=v_ps[:, t, :],
                    lhsT=x_codes[w][:, t, :].bitcast(FP8X4),
                    lhsT_scale=x_scales[w][:, t, :],
                    rhs=wv_codes[:, h, :].bitcast(FP8X4),
                    rhs_scale=wv_scales[:, h, :],
                    start=True,
                    stop=True,
                )
            if h == 0:
                v_grouped[w] = prep.tile([P, H, HD, PACK], BF16, name="v_grouped", align_bytes=64)
            return True, lambda: nc.scalar.copy(out=v_grouped[w][:, h], in_=v_ps[:].rearrange("p t d -> p d t"))

        def quantise_x(w):
            quantise(x_grouped[w][:], x_codes[w][:], x_scales[w][:])

        def quantise_v(w):
            quantise(v_grouped[w][:], v_codes[w][:], v_scales[w][:])

        def banks_of(n):
            if n < ROUNDS_0:
                return [(0, (BANKS * n) // H, (BANKS * n) % H + i, 0) for i in range(BANKS)]
            w, tile = (n - ROUNDS_0) // ROUNDS + 1, (n - ROUNDS_0) % ROUNDS
            return [(w, tile // H, tile % H, kw) for kw in (0, w)]

        s_ps = {}
        row_max = {}
        bias = {}
        sums = {}
        e = {}
        e_flipped = {}
        e_grouped = {}
        e_codes = {}
        e_scales = {}
        o_ps = {}
        total = {}
        inverse = {}

        def score(n, i):
            w, j, h, kw = banks_of(n)[i]
            s_ps[n, i] = psum_s.tile([P, W], F32, name="s_ps", tag="bank")
            nc.tensor.matmul(
                out=s_ps[n, i][:],
                lhsT=qkT[w][:, h, 0, j * P : (j + 1) * P],
                rhs=qkT[kw][:, h, 1, :],
                start=True,
                stop=True,
            )

        def row_maximum(n, i):
            if i == 0:
                row_max[n] = small.tile([P, BANKS], F32, name="row_max")
            nc.vector.tensor_reduce(out=row_max[n][:, i : i + 1], in_=s_ps[n, i][:], axis=AXIS_X, op=MAX)

        def exp_bias(n):
            if n < ROUNDS_0:
                bias[n] = small.tile([P, BANKS], F32, name="bias")
                nc.gpsimd.tensor_scalar(
                    out=bias[n][:], in0=row_max[n][:], scalar1=-SCALE, scalar2=None, op0=MULT
                )
                return
            bias[n] = small.tile([P, 1], F32, name="bias")
            nc.gpsimd.tensor_scalar(
                out=bias[n][:],
                in0=row_max[n][:, 0:1],
                scalar1=row_max[n][:, 1:2],
                scalar2=-SCALE,
                op0=MAX,
                op1=MULT,
            )

        def exponential(n, i):
            w, j, h, kw = banks_of(n)[i]
            if i == 0:
                e[n] = work.tile([P, BANKS, W], BF16, name="e")
                if h == 0:
                    sums[w, j] = small.tile([P, BANKS, H], F32, name="sums")
            source = 0 if w == 0 else i
            column = i if w == 0 else 0
            nc.scalar.activation(
                out=e[n][:, i, :],
                in_=s_ps[n, i][:],
                func=EXP,
                bias=bias[n][:, column : column + 1],
                scale=SCALE,
                accum_out=sums[w, j][:, source, h : h + 1],
            )

        def flip_e(n):
            e_flipped[n] = flip_words(psum_e, e[n][:])

        def regroup_e(n):
            e_grouped[n] = work.tile([P, BANKS, P, PACK], BF16, name="e_grouped", align_bytes=64)
            regroup_words(nc.scalar.copy, e_flipped[n], e_grouped[n][:])

        def quantise_e(n):
            e_codes[n] = work.tile([P, BANKS, P], U32, name="e_codes", align_bytes=64)
            e_scales[n] = work.tile([P, BANKS, P], U8, name="e_scales", align_bytes=64)
            quantise(e_grouped[n][:], e_codes[n][:], e_scales[n][:])

        def weigh_values(n):
            for i, (w, j, h, kw) in enumerate(banks_of(n)):
                if h == 0 and kw == 0:
                    o_ps[w, j] = psum_o.tile([P, H, HD], F32, name="o_ps", tag="bank")
                nc.tensor.matmul_mx(
                    out=o_ps[w, j][:, h, :],
                    lhsT=e_codes[n][:, i, :].bitcast(FP8X4),
                    lhsT_scale=e_scales[n][:, i, :],
                    rhs=v_codes[kw][:, h, :].bitcast(FP8X4),
                    rhs_scale=v_scales[kw][:, h, :],
                    start=(kw == 0),
                    stop=(kw == w),
                )

        def add_sums(w, j):
            if w > 0:
                total[w, j] = small.tile([P, H], F32, name="total")
                nc.gpsimd.tensor_tensor(
                    out=total[w, j][:], in0=sums[w, j][:, 0], in1=sums[w, j][:, 1], op=ADD
                )

        def invert_sums(w, j):
            inverse[w, j] = small.tile([P, H], F32, name="inverse")
            nc.vector.reciprocal(out=inverse[w, j][:], in_=sums[w, j][:, 0] if w == 0 else total[w, j][:])

        def divide_and_store(w, j):
            o_sb = work.tile([P, H, HD], F32)
            nc.vector.tensor_tensor(
                out=o_sb[:],
                in0=o_ps[w, j][:],
                in1=inverse[w, j][:].unsqueeze(2).to_broadcast([P, H, HD]),
                op=MULT,
            )
            nc.sync.dma_start(
                out=out[0, w * W : (w + 1) * W, :].rearrange("(p j) f -> j p f", j=TILES)[j],
                in_=o_sb[:].rearrange("p h d -> p (h d)"),
            )

        wv_raw = const.tile([P, TILES, D], BF16)
        load_qk(0, range(BANKS))
        load_x(0)
        for half in range(2):
            nc.sync.dma_start(
                out=wv_raw[:, 2 * half : 2 * half + 2, :],
                in_=Wv[2 * half * P : 2 * (half + 1) * P, :].rearrange("(o p) f -> p o f", p=P),
            )
        load_qk(0, range(BANKS, H))
        load_x(1)
        load_qk(1, range(H))
        wv_codes = const.tile([P, TILES, P], U32, align_bytes=64)
        wv_scales = const.tile([P, TILES, P], U8, align_bytes=64)
        x_grouped[0] = prep.tile([P, TILES, P, PACK], BF16, name="x_grouped", align_bytes=64)
        wv_grouped = prep.tile([P, TILES, P, PACK], BF16, name="v_grouped", align_bytes=64)
        turn_qk(0, 0)[1]()
        turn_qk(0, 1, psum_e)[1]()
        for rows, grouped, codes, scales in (
            (x_raw[0], x_grouped[0], x_codes[0], x_scales[0]),
            (wv_raw, wv_grouped, wv_codes, wv_scales),
        ):
            halves = (slice(0, 2), slice(2, 4))
            flips = [flip_words(psum_s, rows[:, t, :]) for t in halves]
            if rows is wv_raw:
                keeps = [turn_qk(0, 2), turn_qk(0, 3, psum_e)]
            else:
                for i in range(BANKS):
                    score(0, i)
                    row_maximum(0, i)
                exp_bias(0)
            for flipped, t in zip(flips, halves):
                regroup_words(nc.scalar.copy, flipped, grouped[:, t])
                quantise(grouped[:, t], codes[:, t], scales[:, t])
        copies = [project_v(0, 0, psum_o)]
        for on_scalar, keep_qk in keeps:
            keep_qk()
        for i in range(BANKS):
            exponential(0, i)
        copies += [project_v(0, 1), project_v(0, 2, psum_e)]
        for i in range(BANKS):
            score(1, i)
            row_maximum(1, i)
        exp_bias(1)
        score(2, 0)
        copies[0][1]()
        copies.append(project_v(0, 3, psum_o))
        for on_scalar, copy_v in copies[1:]:
            copy_v()
        quantise_v(0)

        chains = {}
        quantises = {}

        def plan(chain, w, i, wanted):
            n = wanted
            while n in chains:
                n += 1
            chains[n] = (chain, w, i)
            return n

        for w in range(1, NW):
            begin = first_round(w)
            for h in range(H):
                plan(turn_qk, w, h, begin - ROUNDS + 4 * h if w > 1 else 2 * h + 1)
            n = plan(flip_x, w, 0, max(begin - 27, 0))
            n = plan(flip_x, w, 1, max(begin - 23, n + 1))
            quantises[max(begin - 19, n)] = (quantise_x, w)
            n = max(begin - 19, n)
            for h in range(H):
                n = plan(project_v, w, h, max(begin - 13 + 4 * h, n + 1))
            quantises[n + 1 if w == 1 else n + 2] = (quantise_v, w)

        LAST = N_ROUNDS - 1

        def has(n):
            return 0 <= n < N_ROUNDS

        for n in range(0, N_ROUNDS + 3):
            for w in range(2, NW):
                if n == max(first_round(w) - 32, 0):
                    load_x(w)
                if n == first_round(w) - 24:
                    load_qk(w, range(H))

            if has(n - 1) and n <= LAST:
                flip_e(n - 1)
            copy = None
            if n in chains:
                chain, for_w, i = chains[n]
                on_scalar, copy = chain(for_w, i)
            if has(n) and n > 0:
                exponential(n, 0)
            if n == LAST:
                end_flips = [flip_words(psum_s, e[n][:, 0:1])]
            if has(n + 2):
                score(n + 2, 1)
            if has(n - 3):
                weigh_values(n - 3)
            if has(n) and n > 0:
                exponential(n, 1)
            if n == LAST:
                end_flips.append(flip_words(psum_s, e[n][:, 1:2]))
            if has(n + 3):
                score(n + 3, 0)

            finished = None
            if has(n - 3):
                w, j, h, kw = banks_of(n - 3)[1]
                if h == H - 1:
                    finished = w, j
                    if n - 3 < LAST:
                        invert_sums(w, j)
            if has(n + 2):
                row_maximum(n + 2, 0)
            if n == LAST + 1:
                e_grouped[LAST] = work.tile([P, BANKS, P, PACK], BF16, name="e_grouped", align_bytes=64)
                e_codes[LAST] = work.tile([P, BANKS, P], U32, name="e_codes", align_bytes=64)
                e_scales[LAST] = work.tile([P, BANKS, P], U8, name="e_scales", align_bytes=64)
                regroup_words(nc.vector.tensor_copy, end_flips[0], e_grouped[LAST][:, 0:1])
                w, j, h, kw = banks_of(LAST)[1]
                invert_sums(w, j)
            if has(n - 2) and n < LAST + 2:
                quantise_e(n - 2)
            if n == LAST + 1:
                regroup_words(nc.scalar.copy, end_flips[1], e_grouped[LAST][:, 1:2])
                for i in range(BANKS):
                    t = slice(i, i + 1)
                    quantise(e_grouped[LAST][:, t], e_codes[LAST][:, t], e_scales[LAST][:, t])
            if copy and not on_scalar:
                copy()
            if has(n + 2):
                row_maximum(n + 2, 1)
                exp_bias(n + 2)
            if finished:
                divide_and_store(*finished)

            if has(n - 1) and n <= LAST:
                regroup_e(n - 1)
            if copy and on_scalar:
                copy()
            if has(n):
                w, j, h, kw = banks_of(n)[1]
                if h == H - 1:
                    add_sums(w, j)

            if n in quantises:
                step, for_w = quantises[n]
                step(for_w)
